import numpy as np
import ml_dtypes


def mxq(x, axis, fmt="e4m3"):
    dtype, down = {"e4m3": (ml_dtypes.float8_e4m3fn, 7), "e5m2": (ml_dtypes.float8_e5m2, 14)}[fmt]
    v = np.moveaxis(np.asarray(x, np.float32).astype(ml_dtypes.bfloat16).astype(np.float64), axis, -1)
    blocks = v.reshape(v.shape[:-1] + (-1, 32))
    amax = np.abs(blocks).max(-1, keepdims=True)
    byte = np.maximum(np.where(amax > 0, np.frexp(amax)[1] - 1 + 127, 0) - down, 1)
    scale = np.exp2(byte - 127.0)
    codes = (blocks / scale).astype(np.float32).astype(dtype).astype(np.float64)
    return np.moveaxis((codes * scale).reshape(v.shape), -1, axis)


WIDE = False


def mx_kscale(k):
    if not WIDE:
        return np.ones(k)
    levels = np.array([10, -10, 5, -5, 0])
    a = np.random.permutation(np.resize(levels, k // 512 * 4)).reshape(k // 512, 4)
    idx = np.arange(k)
    return np.exp2(a[idx // 512, idx % 128 // 32])


BF16 = ml_dtypes.bfloat16


def bf(x):
    return np.asarray(x, np.float32).astype(BF16)


def f64(x):
    return np.asarray(x).astype(np.float64)


K1, K2 = 3, 3
DIL = 1
PAD = (DIL * (K1 - 1) // 2, DIL * (K2 - 1) // 2)
B, CIN, COUT, H, W = 4, 512, 128, 32, 32


def _unfold(x, k1, k2, dilation, padding):
    b, c, h, w = x.shape
    p0, p1 = padding
    xp = np.pad(x, ((0, 0), (0, 0), (p0, p0), (p1, p1)))
    cols = []
    for i in range(k1):
        for j in range(k2):
            cols.append(xp[:, :, i * dilation:i * dilation + h, j * dilation:j * dilation + w])
    patches = np.stack(cols, axis=2)
    return patches.reshape(b, c, k1 * k2, h * w)


def setup_inputs():
    s = mx_kscale(CIN)
    return {"x": bf(np.random.standard_normal((B, CIN, H, W)) * s[None, :, None, None]),
            "mask": bf(np.random.random((1, K1 * K2, H * W))),
            "weight": bf(np.random.standard_normal((COUT, CIN, K1, K2)) * 0.03 / s[None, :, None, None]),
            "bias": bf(np.random.standard_normal(COUT) * 0.5)}


def reference(x, mask, weight, bias):
    x, mask, weight, bias = f64(x), f64(mask), f64(weight), f64(bias)
    b, cin, h, w = x.shape
    cout = weight.shape[0]
    kk = K1 * K2
    patches = _unfold(x, K1, K2, DIL, PAD)
    patches = patches * mask[:, None, :, :]
    wm = weight.reshape(cout, cin, kk).transpose(0, 2, 1).reshape(cout, kk * cin)
    pm = patches.transpose(0, 2, 1, 3).reshape(b, kk * cin, h * w)
    out = mxq(wm, 1, "e4m3") @ mxq(pm, 1, "e4m3")
    out = out + bias[None, :, None]
    return out.reshape(b, cout, h, w)

@@ -1,0 +1,205 @@
+from contextlib import ExitStack
+
+import concourse.mybir as mybir
+from concourse.masks import make_identity
+
+BF16 = mybir.dt.bfloat16
+F32 = mybir.dt.float32
+U32 = mybir.dt.uint32
+U8 = mybir.dt.uint8
+FP8X4 = mybir.dt.float8_e4m3fn_x4
+MULT = mybir.AluOpType.mult
+IDENT = mybir.ActivationFunctionType.Identity
+
+P = 128
+B, CIN, COUT, H, W = 4, 512, 128, 32, 32
+TAPS = 9
+PIX = H * W
+PACK = 4
+ROW = (W + 4) * PACK
+XG = 4928
+FLOPS = 2 * B * COUT * CIN * TAPS * PIX
+
+
+def tile_input_masked_conv2d_kernel(tc, x, mask, weight, bias, out):
+    nc = tc.nc
+    with ExitStack() as ctx:
+        const = ctx.enter_context(tc.tile_pool(name="const", bufs=1))
+        xr_pool = ctx.enter_context(tc.tile_pool(name="xr", bufs=2))
+        prod_pool = ctx.enter_context(tc.tile_pool(name="prod", bufs=3))
+        code_pool = ctx.enter_context(tc.tile_pool(name="code", bufs=4))
+        out_pool = ctx.enter_context(tc.tile_pool(name="outp", bufs=4))
+        psum = ctx.enter_context(tc.psum_pool(name="psum", bufs=1))
+
+        mask_flat = mask.rearrange("a k n -> (a k n)")
+        mb = const.tile([P, TAPS * PIX], BF16, name="mb")
+        me = [const.tile([P, PIX * PACK], BF16, name="me%d" % k) for k in range(TAPS)]
+        xg = [const.tile([P, XG], BF16, name="xg%d" % b, align_bytes=64) for b in range(B)]
+        w_raw = const.tile([P, CIN * TAPS], BF16, name="w_raw")
+        wg = const.tile([P, TAPS * COUT * PACK], BF16, name="wg", align_bytes=64)
+        wc = const.tile([P, TAPS * COUT], U32, name="wc", align_bytes=64)
+        ws = const.tile([P, TAPS * COUT], U8, name="ws", align_bytes=64)
+        ident = const.tile([P, P], BF16, name="ident")
+        b_bf = const.tile([P, 1], BF16, name="b_bf")
+        b_col = const.tile([P, 1], F32, name="b_col")
+
+        def load_mask(k0, k1):
+            nc.sync.dma_start(
+                out=mb[:, k0 * PIX : k1 * PIX],
+                in_=mask_flat[k0 * PIX : k1 * PIX].partition_broadcast(P),
+            )
+
+        xr = []
+
+        def load_x(b, chunks):
+            t = xr_pool.tile([P, PACK, PIX], BF16, name="xr")
+            xr.append(t)
+            src = x[b].rearrange("(p t) y z -> p t (y z)", t=PACK)
+            step = PIX // chunks
+            for c in range(chunks):
+                nc.sync.dma_start(
+                    out=t[:, :, c * step : (c + 1) * step],
+                    in_=src[:, :, c * step : (c + 1) * step],
+                )
+
+        def zero_pads(b):
+            t = xg[b]
+            nc.vector.memset(
+                t[:, 0 : (H + 2) * ROW].rearrange("p (y r) -> p y r", r=ROW)[:, :, 0:16], 0.0
+            )
+            nc.vector.memset(t[:, 16:ROW], 0.0)
+            nc.vector.memset(t[:, (H + 1) * ROW + 16 : XG], 0.0)
+
+        def regroup(on_vector, b, y0, y1):
+            dst = (
+                xg[b][:, ROW + 16 + y0 * ROW : ROW + 16 + y1 * ROW]
+                .rearrange("p (y r) -> p y r", r=ROW)[:, :, 0 : W * PACK]
+                .rearrange("p y (z t) -> p y z t", t=PACK)
+            )
+            src = xr[b][:, :, y0 * W : y1 * W].rearrange("p t (y z) -> p y z t", z=W)
+            if on_vector:
+                nc.vector.tensor_copy(out=dst, in_=src)
+            else:
+                nc.scalar.copy(out=dst, in_=src)
+
+        def expand(on_vector, k, n0, n1):
+            dst = me[k][:, n0 * PACK : n1 * PACK].rearrange("p (n t) -> p n t", t=PACK)
+            src = mb[:, k * PIX + n0 : k * PIX + n1].unsqueeze(2).to_broadcast([P, n1 - n0, PACK])
+            if on_vector:
+                nc.vector.tensor_copy(out=dst, in_=src)
+            else:
+                nc.scalar.copy(out=dst, in_=src)
+
+        w4 = w_raw[:].rearrange("o (p t k) -> o p t k", t=PACK, k=TAPS)
+
+        def weights(g):
+            taps = [k for k in (2 * g, 2 * g + 1) if k < TAPS]
+            n = len(taps)
+            wt = psum.tile([P, 2 * PACK, COUT], BF16, name="wt", tag="bank%d" % (4 + g % 4))
+            for a, k in enumerate(taps):
+                for t in range(PACK):
+                    nc.tensor.transpose(wt[:, a * PACK + t, :], w4[:, :, t, k], ident[:])
+            lo = 2 * g * COUT * PACK
+            hi = lo + n * COUT * PACK
+            nc.scalar.copy(
+                out=wg[:, lo:hi].rearrange("p (a o t) -> p a o t", a=n, t=PACK),
+                in_=wt[:, 0 : n * PACK, :].rearrange("p (a t) o -> p a o t", t=PACK),
+            )
+            nc.vector.quantize_mx(
+                out=wc[:, lo // PACK : hi // PACK].bitcast(FP8X4),
+                scales=ws[:, lo // PACK : hi // PACK],
+                in_=wg[:, lo:hi],
+            )
+
+        def multiply(k, b):
+            i, j = k // 3, k % 3
+            off = i * ROW + (3 + j) * PACK
+            prod = prod_pool.tile([P, PIX * PACK], BF16, name="prod", align_bytes=64)
+            nc.vector.tensor_tensor(
+                out=prod[:].rearrange("p (y r) -> p y r", r=W * PACK),
+                in0=xg[b][:, off : off + H * ROW].rearrange("p (y r) -> p y r", r=ROW)[:, :, 0 : W * PACK],
+                in1=me[k][:].rearrange("p (y r) -> p y r", r=W * PACK),
+                op=MULT,
+            )
+            return prod
+
+        acc = {}
+
+        def quantise_and_multiply(k, b, prod):
+            codes = code_pool.tile([P, PIX], U32, name="codes", align_bytes=64)
+            scl = code_pool.tile([P, PIX], U8, name="scl", align_bytes=64)
+            nc.vector.quantize_mx(out=codes[:].bitcast(FP8X4), scales=scl[:], in_=prod[:])
+            for h in range(2):
+                if k == 0:
+                    acc[(b, h)] = psum.tile([P, 512], F32, name="acc", tag="bank%d" % (2 * b + h))
+                cols = slice(h * 512, (h + 1) * 512)
+                nc.tensor.matmul_mx(
+                    out=acc[(b, h)][:],
+                    lhsT=wc[:, k * COUT : (k + 1) * COUT].bitcast(FP8X4),
+                    lhsT_scale=ws[:, k * COUT : (k + 1) * COUT],
+                    rhs=codes[:, cols].bitcast(FP8X4),
+                    rhs_scale=scl[:, cols],
+                    start=(k == 0),
+                    stop=(k == TAPS - 1),
+                )
+
+        def finish(b, split):
+            dst = out[b].rearrange("o y z -> o (y z)")
+            for h in range(2):
+                res = out_pool.tile([P, 512], F32, name="res")
+                if split and h == 1:
+                    nc.vector.tensor_scalar_add(out=res[:], in0=acc[(b, h)][:], scalar1=b_col[:, 0:1])
+                else:
+                    nc.scalar.activation(out=res[:], in_=acc[(b, h)][:], func=IDENT, bias=b_col[:, 0:1], scale=1.0)
+                nc.sync.dma_start(out=dst[:, h * 512 : (h + 1) * 512], in_=res[:])
+
+        load_mask(0, 1)
+        load_x(0, 4)
+        load_x(1, 1)
+        nc.sync.dma_start(out=w_raw[:], in_=weight.rearrange("o c i j -> o (c i j)"))
+        load_mask(1, 3)
+        load_mask(3, TAPS)
+        with nc.allow_non_contiguous_dma(reason="128 bias values, one to a partition"):
+            nc.sync.dma_start(out=b_bf[:], in_=bias.rearrange("(o u) -> o u", u=1))
+
+        make_identity(nc, ident[:])
+        for b in range(B):
+            zero_pads(b)
+
+        expand(False, 0, 0, 512)
+        expand(True, 0, 512, PIX)
+        for c in range(4):
+            regroup(True, 0, 8 * c, 8 * c + 8)
+        regroup(False, 1, 0, 11)
+        regroup(True, 1, 11, H)
+        nc.vector.tensor_copy(out=b_col[:], in_=b_bf[:])
+        load_x(2, 1)
+        load_x(3, 1)
+
+        weights(0)
+        expand(False, 1, 0, PIX)
+        weights(1)
+        expand(False, 2, 0, PIX)
+        weights(2)
+        weights(3)
+        expand(False, 3, 0, PIX)
+        weights(4)
+        expand(False, 4, 0, PIX)
+        regroup(False, 2, 0, H)
+        expand(False, 5, 0, PIX)
+        expand(False, 6, 0, PIX)
+        regroup(False, 3, 0, H)
+        expand(False, 7, 0, PIX)
+        expand(False, 8, 0, PIX)
+
+        units = [(k, b) for pair in range(2) for k in range(TAPS) for b in (2 * pair, 2 * pair + 1)]
+        waiting = None
+        for k, b in units:
+            prod = multiply(k, b)
+            if waiting is not None:
+                quantise_and_multiply(*waiting)
+                if waiting[0] == TAPS - 1:
+                    finish(waiting[1], False)
+            waiting = (k, b, prod)
+        quantise_and_multiply(*waiting)
+        finish(waiting[1], True)

@@ -16,6 +16,7 @@ B, CIN, COUT, H, W = 4, 512, 128, 32, 32
 TAPS = 9
 PIX = H * W
 PACK = 4
+LINE = W * PACK
 ROW = (W + 4) * PACK
 XG = 4928
 FLOPS = 2 * B * COUT * CIN * TAPS * PIX
@@ -25,16 +26,16 @@ def tile_input_masked_conv2d_kernel(tc, x, mask, weight, bias, out):
     nc = tc.nc
     with ExitStack() as ctx:
         const = ctx.enter_context(tc.tile_pool(name="const", bufs=1))
-        xr_pool = ctx.enter_context(tc.tile_pool(name="xr", bufs=2))
-        prod_pool = ctx.enter_context(tc.tile_pool(name="prod", bufs=3))
-        code_pool = ctx.enter_context(tc.tile_pool(name="code", bufs=4))
+        xr_pool = ctx.enter_context(tc.tile_pool(name="xr", bufs=4))
+        code_pool = ctx.enter_context(tc.tile_pool(name="code", bufs=6))
         out_pool = ctx.enter_context(tc.tile_pool(name="outp", bufs=4))
         psum = ctx.enter_context(tc.psum_pool(name="psum", bufs=1))
 
         mask_flat = mask.rearrange("a k n -> (a k n)")
         mb = const.tile([P, TAPS * PIX], BF16, name="mb")
-        me = [const.tile([P, PIX * PACK], BF16, name="me%d" % k) for k in range(TAPS)]
+        me = [const.tile([P, PIX * 2], BF16, name="me%d" % k) for k in range(TAPS)]
         xg = [const.tile([P, XG], BF16, name="xg%d" % b, align_bytes=64) for b in range(B)]
+        prods = [const.tile([P, (H + 2) * LINE], BF16, name="prod%d" % n, align_bytes=64) for n in range(3)]
         w_raw = const.tile([P, CIN * TAPS], BF16, name="w_raw")
         wg = const.tile([P, TAPS * COUT * PACK], BF16, name="wg", align_bytes=64)
         wc = const.tile([P, TAPS * COUT], U32, name="wc", align_bytes=64)
@@ -73,7 +74,7 @@ def tile_input_masked_conv2d_kernel(tc, x, mask, weight, bias, out):
         def regroup(on_vector, b, y0, y1):
             dst = (
                 xg[b][:, ROW + 16 + y0 * ROW : ROW + 16 + y1 * ROW]
-                .rearrange("p (y r) -> p y r", r=ROW)[:, :, 0 : W * PACK]
+                .rearrange("p (y r) -> p y r", r=ROW)[:, :, 0:LINE]
                 .rearrange("p y (z t) -> p y z t", t=PACK)
             )
             src = xr[b][:, :, y0 * W : y1 * W].rearrange("p t (y z) -> p y z t", z=W)
@@ -82,13 +83,11 @@ def tile_input_masked_conv2d_kernel(tc, x, mask, weight, bias, out):
             else:
                 nc.scalar.copy(out=dst, in_=src)
 
-        def expand(on_vector, k, n0, n1):
-            dst = me[k][:, n0 * PACK : n1 * PACK].rearrange("p (n t) -> p n t", t=PACK)
-            src = mb[:, k * PIX + n0 : k * PIX + n1].unsqueeze(2).to_broadcast([P, n1 - n0, PACK])
-            if on_vector:
-                nc.vector.tensor_copy(out=dst, in_=src)
-            else:
-                nc.scalar.copy(out=dst, in_=src)
+        def expand(k, n0, n1):
+            nc.scalar.copy(
+                out=me[k][:, n0 * 2 : n1 * 2].rearrange("p (n e) -> p n e", e=2),
+                in_=mb[:, k * PIX + n0 : k * PIX + n1].unsqueeze(2).to_broadcast([P, n1 - n0, 2]),
+            )
 
         w4 = w_raw[:].rearrange("o (p t k) -> o p t k", t=PACK, k=TAPS)
 
@@ -111,95 +110,128 @@ def tile_input_masked_conv2d_kernel(tc, x, mask, weight, bias, out):
                 in_=wg[:, lo:hi],
             )
 
-        def multiply(k, b):
+        def multiply(n, k, b, y0, y1):
             i, j = k // 3, k % 3
+            y0 = max(y0, 1 - i)
+            y1 = min(y1, H + 1 - i)
             off = i * ROW + (3 + j) * PACK
-            prod = prod_pool.tile([P, PIX * PACK], BF16, name="prod", align_bytes=64)
             nc.vector.tensor_tensor(
-                out=prod[:].rearrange("p (y r) -> p y r", r=W * PACK),
-                in0=xg[b][:, off : off + H * ROW].rearrange("p (y r) -> p y r", r=ROW)[:, :, 0 : W * PACK],
-                in1=me[k][:].rearrange("p (y r) -> p y r", r=W * PACK),
+                out=prods[n][:, (i + y0) * LINE : (i + y1) * LINE].rearrange(
+                    "p (y z r e) -> p y z r e", z=W, r=2, e=2
+                ),
+                in0=xg[b][:, off + y0 * ROW : off + y1 * ROW]
+                .rearrange("p (y q) -> p y q", q=ROW)[:, :, 0:LINE]
+                .rearrange("p y (z r e) -> p y z r e", r=2, e=2),
+                in1=me[k][:, y0 * W * 2 : y1 * W * 2]
+                .rearrange("p (y z e) -> p y z e", z=W, e=2)
+                .unsqueeze(3)
+                .to_broadcast([P, y1 - y0, W, 2, 2]),
                 op=MULT,
             )
-            return prod
 
         acc = {}
+        held = {}
 
-        def quantise_and_multiply(k, b, prod):
-            codes = code_pool.tile([P, PIX], U32, name="codes", align_bytes=64)
-            scl = code_pool.tile([P, PIX], U8, name="scl", align_bytes=64)
-            nc.vector.quantize_mx(out=codes[:].bitcast(FP8X4), scales=scl[:], in_=prod[:])
-            for h in range(2):
-                if k == 0:
-                    acc[(b, h)] = psum.tile([P, 512], F32, name="acc", tag="bank%d" % (2 * b + h))
-                cols = slice(h * 512, (h + 1) * 512)
-                nc.tensor.matmul_mx(
-                    out=acc[(b, h)][:],
-                    lhsT=wc[:, k * COUT : (k + 1) * COUT].bitcast(FP8X4),
-                    lhsT_scale=ws[:, k * COUT : (k + 1) * COUT],
-                    rhs=codes[:, cols].bitcast(FP8X4),
-                    rhs_scale=scl[:, cols],
-                    start=(k == 0),
-                    stop=(k == TAPS - 1),
-                )
+        def quantise(n, k, b, part, parts):
+            if part == 0:
+                codes = code_pool.tile([P, PIX], U32, name="codes", align_bytes=64)
+                scl = code_pool.tile([P, PIX], U8, name="scl", align_bytes=64)
+                held[(k, b)] = (codes, scl)
+            codes, scl = held[(k, b)]
+            i = k // 3
+            wid = PIX // parts
+            nc.vector.quantize_mx(
+                out=codes[:, part * wid : (part + 1) * wid].bitcast(FP8X4),
+                scales=scl[:, part * wid : (part + 1) * wid],
+                in_=prods[n][:, i * LINE + part * wid * PACK : i * LINE + (part + 1) * wid * PACK],
+            )
 
-        def finish(b, split):
-            dst = out[b].rearrange("o y z -> o (y z)")
-            for h in range(2):
-                res = out_pool.tile([P, 512], F32, name="res")
-                if split and h == 1:
-                    nc.vector.tensor_scalar_add(out=res[:], in0=acc[(b, h)][:], scalar1=b_col[:, 0:1])
-                else:
-                    nc.scalar.activation(out=res[:], in_=acc[(b, h)][:], func=IDENT, bias=b_col[:, 0:1], scale=1.0)
-                nc.sync.dma_start(out=dst[:, h * 512 : (h + 1) * 512], in_=res[:])
+        def matmul(k, b, h):
+            codes, scl = held[(k, b)]
+            if k == 0:
+                acc[(b, h)] = psum.tile([P, 512], F32, name="acc", tag="bank%d" % (2 * b + h))
+            cols = slice(h * 512, (h + 1) * 512)
+            nc.tensor.matmul_mx(
+                out=acc[(b, h)][:],
+                lhsT=wc[:, k * COUT : (k + 1) * COUT].bitcast(FP8X4),
+                lhsT_scale=ws[:, k * COUT : (k + 1) * COUT],
+                rhs=codes[:, cols].bitcast(FP8X4),
+                rhs_scale=scl[:, cols],
+                start=(k == 0),
+                stop=(k == TAPS - 1),
+            )
+
+        def finish(b, h):
+            res = out_pool.tile([P, 512], F32, name="res")
+            nc.scalar.activation(out=res[:], in_=acc[(b, h)][:], func=IDENT, bias=b_col[:, 0:1], scale=1.0)
+            nc.sync.dma_start(out=out[b].rearrange("o y z -> o (y z)")[:, h * 512 : (h + 1) * 512], in_=res[:])
 
         load_mask(0, 1)
         load_x(0, 4)
-        load_x(1, 1)
+        load_x(1, 4)
         nc.sync.dma_start(out=w_raw[:], in_=weight.rearrange("o c i j -> o (c i j)"))
         load_mask(1, 3)
         load_mask(3, TAPS)
         with nc.allow_non_contiguous_dma(reason="128 bias values, one to a partition"):
             nc.sync.dma_start(out=b_bf[:], in_=bias.rearrange("(o u) -> o u", u=1))
+        load_x(2, 1)
+        load_x(3, 1)
 
         make_identity(nc, ident[:])
         for b in range(B):
             zero_pads(b)
+        for n in range(3):
+            nc.vector.memset(prods[n][:, 0:LINE], 0.0)
+            nc.vector.memset(prods[n][:, (H + 1) * LINE : (H + 2) * LINE], 0.0)
 
-        expand(False, 0, 0, 512)
-        expand(True, 0, 512, PIX)
-        for c in range(4):
-            regroup(True, 0, 8 * c, 8 * c + 8)
-        regroup(False, 1, 0, 11)
-        regroup(True, 1, 11, H)
+        for q in range(4):
+            expand(0, 256 * q, 256 * q + 256)
+        for q in range(4):
+            regroup(True, 0, 8 * q, 8 * q + 8)
+            multiply(0, 0, 0, 8 * q, 8 * q + 8)
+        for q in range(3):
+            regroup(False, 1, 8 * q, 8 * q + 8)
+        regroup(True, 1, 24, 32)
         nc.vector.tensor_copy(out=b_col[:], in_=b_bf[:])
-        load_x(2, 1)
-        load_x(3, 1)
 
+        expand(1, 0, PIX)
         weights(0)
-        expand(False, 1, 0, PIX)
         weights(1)
-        expand(False, 2, 0, PIX)
+        expand(2, 0, PIX)
         weights(2)
         weights(3)
-        expand(False, 3, 0, PIX)
         weights(4)
-        expand(False, 4, 0, PIX)
+        expand(3, 0, PIX)
+        expand(4, 0, PIX)
         regroup(False, 2, 0, H)
-        expand(False, 5, 0, PIX)
-        expand(False, 6, 0, PIX)
+        expand(5, 0, PIX)
+        expand(6, 0, PIX)
         regroup(False, 3, 0, H)
-        expand(False, 7, 0, PIX)
-        expand(False, 8, 0, PIX)
+        expand(7, 0, PIX)
+        expand(8, 0, PIX)
 
         units = [(k, b) for pair in range(2) for k in range(TAPS) for b in (2 * pair, 2 * pair + 1)]
-        waiting = None
-        for k, b in units:
-            prod = multiply(k, b)
-            if waiting is not None:
-                quantise_and_multiply(*waiting)
-                if waiting[0] == TAPS - 1:
-                    finish(waiting[1], False)
-            waiting = (k, b, prod)
-        quantise_and_multiply(*waiting)
-        finish(waiting[1], True)
+        last = len(units) - 1
+        for u, (k, b) in enumerate(units):
+            if u == 1:
+                multiply(u % 3, k, b, 0, 16)
+                multiply(u % 3, k, b, 16, H)
+            elif u == last:
+                multiply(u % 3, k, b, 0, 16)
+            elif u > 1:
+                multiply(u % 3, k, b, 0, H)
+            if u > 0:
+                pk, pb = units[u - 1]
+                quantise((u - 1) % 3, pk, pb, 0, 1)
+                for h in range(2):
+                    matmul(pk, pb, h)
+                    if pk == TAPS - 1:
+                        finish(pb, h)
+        k, b = units[last]
+        quantise(last % 3, k, b, 0, 2)
+        multiply(last % 3, k, b, 16, H)
+        matmul(k, b, 0)
+        finish(b, 0)
+        quantise(last % 3, k, b, 1, 2)
+        matmul(k, b, 1)
+        finish(b, 1)

@@ -10,6 +10,7 @@ U8 = mybir.dt.uint8
 FP8X4 = mybir.dt.float8_e4m3fn_x4
 MULT = mybir.AluOpType.mult
 IDENT = mybir.ActivationFunctionType.Identity
+COPY = mybir.ActivationFunctionType.Copy
 
 P = 128
 B, CIN, COUT, H, W = 4, 512, 128, 32, 32
@@ -19,30 +20,40 @@ PACK = 4
 LINE = W * PACK
 ROW = (W + 4) * PACK
 XG = 4928
+BUF = (H + 2) * LINE
 FLOPS = 2 * B * COUT * CIN * TAPS * PIX
+
+SCALAR_WAY = ((1,), (0, 2, 1))
 
 
 def tile_input_masked_conv2d_kernel(tc, x, mask, weight, bias, out):
     nc = tc.nc
     with ExitStack() as ctx:
         const = ctx.enter_context(tc.tile_pool(name="const", bufs=1))
-        xr_pool = ctx.enter_context(tc.tile_pool(name="xr", bufs=4))
-        code_pool = ctx.enter_context(tc.tile_pool(name="code", bufs=6))
+        xr_pool = ctx.enter_context(tc.tile_pool(name="xr", bufs=2))
+        xm_pool = ctx.enter_context(tc.tile_pool(name="xm", bufs=8))
+        code_pool = ctx.enter_context(tc.tile_pool(name="code", bufs=4))
         out_pool = ctx.enter_context(tc.tile_pool(name="outp", bufs=4))
         psum = ctx.enter_context(tc.psum_pool(name="psum", bufs=1))
 
         mask_flat = mask.rearrange("a k n -> (a k n)")
         mb = const.tile([P, TAPS * PIX], BF16, name="mb")
-        me = [const.tile([P, PIX * 2], BF16, name="me%d" % k) for k in range(TAPS)]
+        me = {}
+        for k in range(TAPS):
+            if k != 4:
+                me[k] = const.tile([P, PIX * 2], BF16, name="me%d" % k)
         xg = [const.tile([P, XG], BF16, name="xg%d" % b, align_bytes=64) for b in range(B)]
-        prods = [const.tile([P, (H + 2) * LINE], BF16, name="prod%d" % n, align_bytes=64) for n in range(3)]
-        w_raw = const.tile([P, CIN * TAPS], BF16, name="w_raw")
-        wg = const.tile([P, TAPS * COUT * PACK], BF16, name="wg", align_bytes=64)
+        prods = [const.tile([P, BUF], BF16, name="prod%d" % n, align_bytes=64) for n in range(3)]
+        w_raw = const.tile([P, CIN * TAPS], BF16, name="w_raw", tag="g0", align_bytes=64)
+        wg = const.tile([P, TAPS * COUT * PACK], BF16, name="wg", tag="g2", align_bytes=64)
         wc = const.tile([P, TAPS * COUT], U32, name="wc", align_bytes=64)
         ws = const.tile([P, TAPS * COUT], U8, name="ws", align_bytes=64)
         ident = const.tile([P, P], BF16, name="ident")
         b_bf = const.tile([P, 1], BF16, name="b_bf")
         b_col = const.tile([P, 1], F32, name="b_col")
+        m_rows = const.tile([P, W], BF16, name="m_rows")
+        m_wide = const.tile([P, LINE], BF16, name="m_wide")
+        m_col = const.tile([P, P], F32, name="m_col")
 
         def load_mask(k0, k1):
             nc.sync.dma_start(
@@ -110,6 +121,15 @@ def tile_input_masked_conv2d_kernel(tc, x, mask, weight, bias, out):
                 in_=wg[:, lo:hi],
             )
 
+        def mask_columns():
+            nc.vector.tensor_copy(
+                out=m_wide[:].rearrange("p (z t) -> p z t", t=PACK),
+                in_=m_rows[:].unsqueeze(2).to_broadcast([P, W, PACK]),
+            )
+            mt = psum.tile([P, P], BF16, name="mt", tag="bank5")
+            nc.tensor.transpose(mt[:], m_wide[:], ident[:])
+            nc.vector.tensor_copy(out=m_col[:], in_=mt[:])
+
         def multiply(n, k, b, y0, y1):
             i, j = k // 3, k % 3
             y0 = max(y0, 1 - i)
@@ -129,27 +149,66 @@ def tile_input_masked_conv2d_kernel(tc, x, mask, weight, bias, out):
                 op=MULT,
             )
 
+        big = {}
+
+        def scalar_way(i, pair):
+            if i not in big:
+                big[i] = const.tile([P, 2, BUF], BF16, name="big%d" % i, tag="g%d" % i, align_bytes=64)
+                if i == 0:
+                    nc.vector.memset(big[i][:, :, 0:LINE], 0.0)
+                if i == 2:
+                    nc.vector.memset(big[i][:, :, (H + 1) * LINE : BUF], 0.0)
+            lo, hi = max(0, i - 1), min(H, H + i - 1)
+            for g in range(H // 4):
+                rows = [s for s in range(4 * g, 4 * g + 4) if lo <= s < hi]
+                xt = psum.tile([P, 4, 2, P], BF16, name="xt", tag="bank%d" % (4 + g % 2))
+                for s in rows:
+                    for a in range(2):
+                        start = (s + 1) * ROW + 16
+                        nc.tensor.transpose(xt[:, s % 4, a, :], xg[2 * pair + a][:, start : start + LINE], ident[:])
+                pt = psum.tile([P, 2, 4, LINE], BF16, name="pt", tag="bank%d" % (6 + g % 2))
+                for s in rows:
+                    xm = xm_pool.tile([P, 2, P], BF16, name="xm")
+                    col = 32 * i + s - i + 1
+                    nc.scalar.activation(out=xm[:], in_=xt[:, s % 4, :, :], func=COPY, scale=m_col[:, col : col + 1])
+                    for a in range(2):
+                        nc.tensor.transpose(pt[:, a, s % 4, :], xm[:, a, :], ident[:])
+                nc.scalar.copy(
+                    out=big[i][:, :, (rows[0] + 1) * LINE : (rows[-1] + 2) * LINE].rearrange(
+                        "p a (s q) -> p a s q", q=LINE
+                    ),
+                    in_=pt[:, :, rows[0] % 4 : rows[-1] % 4 + 1, :],
+                )
+
         acc = {}
         held = {}
+        passes = {}
 
-        def quantise(n, k, b, part, parts):
+        def quantise(src, k, b, part, parts):
             if part == 0:
                 codes = code_pool.tile([P, PIX], U32, name="codes", align_bytes=64)
                 scl = code_pool.tile([P, PIX], U8, name="scl", align_bytes=64)
                 held[(k, b)] = (codes, scl)
             codes, scl = held[(k, b)]
-            i = k // 3
             wid = PIX // parts
             nc.vector.quantize_mx(
                 out=codes[:, part * wid : (part + 1) * wid].bitcast(FP8X4),
                 scales=scl[:, part * wid : (part + 1) * wid],
-                in_=prods[n][:, i * LINE + part * wid * PACK : i * LINE + (part + 1) * wid * PACK],
+                in_=src[:, part * wid * PACK : (part + 1) * wid * PACK],
             )
+
+        def window(n, k):
+            return prods[n][:, (k // 3) * LINE : (k // 3 + H) * LINE]
+
+        def big_window(i, b):
+            return big[i][:, b % 2, i * LINE : (i + H) * LINE]
 
         def matmul(k, b, h):
             codes, scl = held[(k, b)]
-            if k == 0:
-                acc[(b, h)] = psum.tile([P, 512], F32, name="acc", tag="bank%d" % (2 * b + h))
+            seen = passes.get((b, h), 0)
+            passes[(b, h)] = seen + 1
+            if seen == 0:
+                acc[(b, h)] = psum.tile([P, 512], F32, name="acc", tag="bank%d" % (2 * (b % 2) + h))
             cols = slice(h * 512, (h + 1) * 512)
             nc.tensor.matmul_mx(
                 out=acc[(b, h)][:],
@@ -157,32 +216,35 @@ def tile_input_masked_conv2d_kernel(tc, x, mask, weight, bias, out):
                 lhsT_scale=ws[:, k * COUT : (k + 1) * COUT],
                 rhs=codes[:, cols].bitcast(FP8X4),
                 rhs_scale=scl[:, cols],
-                start=(k == 0),
-                stop=(k == TAPS - 1),
+                start=(seen == 0),
+                stop=(seen == TAPS - 1),
             )
-
-        def finish(b, h):
-            res = out_pool.tile([P, 512], F32, name="res")
-            nc.scalar.activation(out=res[:], in_=acc[(b, h)][:], func=IDENT, bias=b_col[:, 0:1], scale=1.0)
-            nc.sync.dma_start(out=out[b].rearrange("o y z -> o (y z)")[:, h * 512 : (h + 1) * 512], in_=res[:])
+            if seen == TAPS - 1:
+                res = out_pool.tile([P, 512], F32, name="res")
+                nc.scalar.activation(out=res[:], in_=acc[(b, h)][:], func=IDENT, bias=b_col[:, 0:1], scale=1.0)
+                nc.sync.dma_start(out=out[b].rearrange("o y z -> o (y z)")[:, cols], in_=res[:])
 
         load_mask(0, 1)
         load_x(0, 4)
         load_x(1, 4)
         nc.sync.dma_start(out=w_raw[:], in_=weight.rearrange("o c i j -> o (c i j)"))
         load_mask(1, 3)
+        nc.vector.memset(m_rows[:], 0.0)
+        for i in range(3):
+            nc.sync.dma_start(
+                out=m_rows[32 * i : 32 * i + 32, :],
+                in_=mask_flat[(3 * i + 1) * PIX : (3 * i + 2) * PIX].rearrange("(y z) -> y z", z=W),
+            )
         load_mask(3, TAPS)
         with nc.allow_non_contiguous_dma(reason="128 bias values, one to a partition"):
             nc.sync.dma_start(out=b_bf[:], in_=bias.rearrange("(o u) -> o u", u=1))
-        load_x(2, 1)
-        load_x(3, 1)
 
         make_identity(nc, ident[:])
         for b in range(B):
             zero_pads(b)
         for n in range(3):
             nc.vector.memset(prods[n][:, 0:LINE], 0.0)
-            nc.vector.memset(prods[n][:, (H + 1) * LINE : (H + 2) * LINE], 0.0)
+            nc.vector.memset(prods[n][:, (H + 1) * LINE : BUF], 0.0)
 
         for q in range(4):
             expand(0, 256 * q, 256 * q + 256)
@@ -193,6 +255,8 @@ def tile_input_masked_conv2d_kernel(tc, x, mask, weight, bias, out):
             regroup(False, 1, 8 * q, 8 * q + 8)
         regroup(True, 1, 24, 32)
         nc.vector.tensor_copy(out=b_col[:], in_=b_bf[:])
+        load_x(2, 1)
+        load_x(3, 1)
 
         expand(1, 0, PIX)
         weights(0)
@@ -201,37 +265,43 @@ def tile_input_masked_conv2d_kernel(tc, x, mask, weight, bias, out):
         weights(2)
         weights(3)
         weights(4)
+        mask_columns()
         expand(3, 0, PIX)
-        expand(4, 0, PIX)
-        regroup(False, 2, 0, H)
         expand(5, 0, PIX)
         expand(6, 0, PIX)
-        regroup(False, 3, 0, H)
+        scalar_way(1, 0)
         expand(7, 0, PIX)
         expand(8, 0, PIX)
+        regroup(False, 2, 0, H)
+        regroup(False, 3, 0, H)
+        scalar_way(0, 1)
+        scalar_way(2, 1)
 
-        units = [(k, b) for pair in range(2) for k in range(TAPS) for b in (2 * pair, 2 * pair + 1)]
-        last = len(units) - 1
-        for u, (k, b) in enumerate(units):
-            if u == 1:
-                multiply(u % 3, k, b, 0, 16)
-                multiply(u % 3, k, b, 16, H)
-            elif u == last:
-                multiply(u % 3, k, b, 0, 16)
-            elif u > 1:
-                multiply(u % 3, k, b, 0, H)
-            if u > 0:
-                pk, pb = units[u - 1]
-                quantise((u - 1) % 3, pk, pb, 0, 1)
-                for h in range(2):
-                    matmul(pk, pb, h)
-                    if pk == TAPS - 1:
-                        finish(pb, h)
-        k, b = units[last]
-        quantise(last % 3, k, b, 0, 2)
-        multiply(last % 3, k, b, 16, H)
-        matmul(k, b, 0)
-        finish(b, 0)
-        quantise(last % 3, k, b, 1, 2)
-        matmul(k, b, 1)
-        finish(b, 1)
+        n = 0
+        waiting = None
+        for pair in range(2):
+            slow = [3 * i + 1 for i in SCALAR_WAY[pair]]
+            for k in [k for k in range(TAPS) if k not in slow]:
+                for b in (2 * pair, 2 * pair + 1):
+                    if n == 1:
+                        multiply(n % 3, k, b, 0, 16)
+                        multiply(n % 3, k, b, 16, H)
+                    elif n > 1:
+                        multiply(n % 3, k, b, 0, H)
+                    if waiting is not None:
+                        quantise(window(waiting[0], waiting[1]), waiting[1], waiting[2], 0, 1)
+                        matmul(waiting[1], waiting[2], 0)
+                        matmul(waiting[1], waiting[2], 1)
+                    waiting = (n % 3, k, b)
+                    n += 1
+            quantise(window(waiting[0], waiting[1]), waiting[1], waiting[2], 0, 1)
+            matmul(waiting[1], waiting[2], 0)
+            matmul(waiting[1], waiting[2], 1)
+            waiting = None
+            for i in SCALAR_WAY[pair]:
+                for b in (2 * pair, 2 * pair + 1):
+                    for h in range(2):
+                        quantise(big_window(i, b), 3 * i + 1, b, h, 2)
+                        matmul(3 * i + 1, b, h)
+            if pair == 0:
+                scalar_way(1, 1)

@@ -23,7 +23,7 @@ XG = 4928
 BUF = (H + 2) * LINE
 FLOPS = 2 * B * COUT * CIN * TAPS * PIX
 
-SCALAR_WAY = ((1,), (0, 2, 1))
+SCALAR_WAY = ((1,), (1, 0))
 
 
 def tile_input_masked_conv2d_kernel(tc, x, mask, weight, bias, out):
@@ -31,8 +31,8 @@ def tile_input_masked_conv2d_kernel(tc, x, mask, weight, bias, out):
     with ExitStack() as ctx:
         const = ctx.enter_context(tc.tile_pool(name="const", bufs=1))
         xr_pool = ctx.enter_context(tc.tile_pool(name="xr", bufs=2))
-        xm_pool = ctx.enter_context(tc.tile_pool(name="xm", bufs=8))
-        code_pool = ctx.enter_context(tc.tile_pool(name="code", bufs=4))
+        xm_pool = ctx.enter_context(tc.tile_pool(name="xm", bufs=4))
+        code_pool = ctx.enter_context(tc.tile_pool(name="code", bufs=6))
         out_pool = ctx.enter_context(tc.tile_pool(name="outp", bufs=4))
         psum = ctx.enter_context(tc.psum_pool(name="psum", bufs=1))
 
@@ -45,7 +45,7 @@ def tile_input_masked_conv2d_kernel(tc, x, mask, weight, bias, out):
         xg = [const.tile([P, XG], BF16, name="xg%d" % b, align_bytes=64) for b in range(B)]
         prods = [const.tile([P, BUF], BF16, name="prod%d" % n, align_bytes=64) for n in range(3)]
         w_raw = const.tile([P, CIN * TAPS], BF16, name="w_raw", tag="g0", align_bytes=64)
-        wg = const.tile([P, TAPS * COUT * PACK], BF16, name="wg", tag="g2", align_bytes=64)
+        wg = const.tile([P, TAPS * COUT * PACK], BF16, name="wg", align_bytes=64)
         wc = const.tile([P, TAPS * COUT], U32, name="wc", align_bytes=64)
         ws = const.tile([P, TAPS * COUT], U8, name="ws", align_bytes=64)
         ident = const.tile([P, P], BF16, name="ident")
@@ -151,34 +151,59 @@ def tile_input_masked_conv2d_kernel(tc, x, mask, weight, bias, out):
 
         big = {}
 
-        def scalar_way(i, pair):
-            if i not in big:
-                big[i] = const.tile([P, 2, BUF], BF16, name="big%d" % i, tag="g%d" % i, align_bytes=64)
-                if i == 0:
-                    nc.vector.memset(big[i][:, :, 0:LINE], 0.0)
-                if i == 2:
-                    nc.vector.memset(big[i][:, :, (H + 1) * LINE : BUF], 0.0)
-            lo, hi = max(0, i - 1), min(H, H + i - 1)
-            for g in range(H // 4):
-                rows = [s for s in range(4 * g, 4 * g + 4) if lo <= s < hi]
-                xt = psum.tile([P, 4, 2, P], BF16, name="xt", tag="bank%d" % (4 + g % 2))
-                for s in rows:
+        def scalar_way(rows_of_kernel, pair):
+            for i in rows_of_kernel:
+                if i not in big:
+                    big[i] = const.tile([P, 2, BUF], BF16, name="big%d" % i, tag="g%d" % i, align_bytes=64)
+                    if i == 0:
+                        nc.vector.memset(big[i][:, :, 0:LINE], 0.0)
+                    if i == 2:
+                        nc.vector.memset(big[i][:, :, (H + 1) * LINE : BUF], 0.0)
+            groups = H // 4
+            xts = {}
+            pts = {}
+
+            def rows(i, g):
+                return [s for s in range(4 * g, 4 * g + 4) if max(0, i - 1) <= s < min(H, H + i - 1)]
+
+            def there(g):
+                xts[g] = psum.tile([P, 4, 2, P], BF16, name="xt", tag="bank%d" % (4 + g % 2))
+                for s in range(4 * g, 4 * g + 4):
                     for a in range(2):
                         start = (s + 1) * ROW + 16
-                        nc.tensor.transpose(xt[:, s % 4, a, :], xg[2 * pair + a][:, start : start + LINE], ident[:])
-                pt = psum.tile([P, 2, 4, LINE], BF16, name="pt", tag="bank%d" % (6 + g % 2))
-                for s in rows:
-                    xm = xm_pool.tile([P, 2, P], BF16, name="xm")
-                    col = 32 * i + s - i + 1
-                    nc.scalar.activation(out=xm[:], in_=xt[:, s % 4, :, :], func=COPY, scale=m_col[:, col : col + 1])
-                    for a in range(2):
-                        nc.tensor.transpose(pt[:, a, s % 4, :], xm[:, a, :], ident[:])
-                nc.scalar.copy(
-                    out=big[i][:, :, (rows[0] + 1) * LINE : (rows[-1] + 2) * LINE].rearrange(
-                        "p a (s q) -> p a s q", q=LINE
-                    ),
-                    in_=pt[:, :, rows[0] % 4 : rows[-1] % 4 + 1, :],
-                )
+                        nc.tensor.transpose(xts[g][:, s % 4, a, :], xg[2 * pair + a][:, start : start + LINE], ident[:])
+
+            def leave(g):
+                for n, i in enumerate(rows_of_kernel):
+                    r = rows(i, g)
+                    nc.scalar.copy(
+                        out=big[i][:, :, (r[0] + 1) * LINE : (r[-1] + 2) * LINE].rearrange(
+                            "p a (s q) -> p a s q", q=LINE
+                        ),
+                        in_=pts[(i, g)][:, :, r[0] % 4 : r[-1] % 4 + 1, :],
+                    )
+
+            there(0)
+            for g in range(groups):
+                if g + 1 < groups:
+                    there(g + 1)
+                xms = {}
+                for i in rows_of_kernel:
+                    xms[i] = xm_pool.tile([P, 4, 2, P], BF16, name="xm")
+                    for s in rows(i, g):
+                        col = 32 * i + s - i + 1
+                        nc.scalar.activation(
+                            out=xms[i][:, s % 4, :, :], in_=xts[g][:, s % 4, :, :], func=COPY, scale=m_col[:, col : col + 1]
+                        )
+                if g > 0:
+                    leave(g - 1)
+                for n, i in enumerate(rows_of_kernel):
+                    bank = 6 + (n if len(rows_of_kernel) == 2 else g % 2)
+                    pts[(i, g)] = psum.tile([P, 2, 4, LINE], BF16, name="pt", tag="bank%d" % bank)
+                    for s in rows(i, g):
+                        for a in range(2):
+                            nc.tensor.transpose(pts[(i, g)][:, a, s % 4, :], xms[i][:, s % 4, a, :], ident[:])
+            leave(groups - 1)
 
         acc = {}
         held = {}
@@ -269,13 +294,11 @@ def tile_input_masked_conv2d_kernel(tc, x, mask, weight, bias, out):
         expand(3, 0, PIX)
         expand(5, 0, PIX)
         expand(6, 0, PIX)
-        scalar_way(1, 0)
+        scalar_way(SCALAR_WAY[0], 0)
         expand(7, 0, PIX)
         expand(8, 0, PIX)
         regroup(False, 2, 0, H)
         regroup(False, 3, 0, H)
-        scalar_way(0, 1)
-        scalar_way(2, 1)
 
         n = 0
         waiting = None
@@ -304,4 +327,4 @@ def tile_input_masked_conv2d_kernel(tc, x, mask, weight, bias, out):
                         quantise(big_window(i, b), 3 * i + 1, b, h, 2)
                         matmul(3 * i + 1, b, h)
             if pair == 0:
-                scalar_way(1, 1)
+                scalar_way(SCALAR_WAY[1], 1)

@@ -23,7 +23,7 @@ XG = 4928
 BUF = (H + 2) * LINE
 FLOPS = 2 * B * COUT * CIN * TAPS * PIX
 
-SCALAR_WAY = ((1,), (1, 0))
+SCALAR_WAY = (((1,),), ((0, 2), (1,)))
 
 
 def tile_input_masked_conv2d_kernel(tc, x, mask, weight, bias, out):
@@ -32,7 +32,7 @@ def tile_input_masked_conv2d_kernel(tc, x, mask, weight, bias, out):
         const = ctx.enter_context(tc.tile_pool(name="const", bufs=1))
         xr_pool = ctx.enter_context(tc.tile_pool(name="xr", bufs=2))
         xm_pool = ctx.enter_context(tc.tile_pool(name="xm", bufs=4))
-        code_pool = ctx.enter_context(tc.tile_pool(name="code", bufs=6))
+        code_pool = ctx.enter_context(tc.tile_pool(name="code", bufs=5))
         out_pool = ctx.enter_context(tc.tile_pool(name="outp", bufs=4))
         psum = ctx.enter_context(tc.psum_pool(name="psum", bufs=1))
 
@@ -45,7 +45,7 @@ def tile_input_masked_conv2d_kernel(tc, x, mask, weight, bias, out):
         xg = [const.tile([P, XG], BF16, name="xg%d" % b, align_bytes=64) for b in range(B)]
         prods = [const.tile([P, BUF], BF16, name="prod%d" % n, align_bytes=64) for n in range(3)]
         w_raw = const.tile([P, CIN * TAPS], BF16, name="w_raw", tag="g0", align_bytes=64)
-        wg = const.tile([P, TAPS * COUT * PACK], BF16, name="wg", align_bytes=64)
+        wg = const.tile([P, TAPS * COUT * PACK], BF16, name="wg", tag="g2", align_bytes=64)
         wc = const.tile([P, TAPS * COUT], U32, name="wc", align_bytes=64)
         ws = const.tile([P, TAPS * COUT], U8, name="ws", align_bytes=64)
         ident = const.tile([P, P], BF16, name="ident")
@@ -63,12 +63,13 @@ def tile_input_masked_conv2d_kernel(tc, x, mask, weight, bias, out):
 
         xr = []
 
-        def load_x(b, chunks):
-            t = xr_pool.tile([P, PACK, PIX], BF16, name="xr")
-            xr.append(t)
+        def load_x(b, chunks, which):
+            if len(xr) == b:
+                xr.append(xr_pool.tile([P, PACK, PIX], BF16, name="xr"))
+            t = xr[b]
             src = x[b].rearrange("(p t) y z -> p t (y z)", t=PACK)
             step = PIX // chunks
-            for c in range(chunks):
+            for c in which:
                 nc.sync.dma_start(
                     out=t[:, :, c * step : (c + 1) * step],
                     in_=src[:, :, c * step : (c + 1) * step],
@@ -166,8 +167,13 @@ def tile_input_masked_conv2d_kernel(tc, x, mask, weight, bias, out):
             def rows(i, g):
                 return [s for s in range(4 * g, 4 * g + 4) if max(0, i - 1) <= s < min(H, H + i - 1)]
 
+            def keep_clock(bank, times):
+                for n in range(times):
+                    nc.tensor.matmul(out=bank[:, 0:256].bitcast(F32), lhsT=m_col[:], rhs=m_col[:], start=True, stop=True)
+
             def there(g):
                 xts[g] = psum.tile([P, 4, 2, P], BF16, name="xt", tag="bank%d" % (4 + g % 2))
+                keep_clock(xts[g][:].rearrange("p s a q -> p (s a q)"), (4 if g == 0 else len(rows_of_kernel)))
                 for s in range(4 * g, 4 * g + 4):
                     for a in range(2):
                         start = (s + 1) * ROW + 16
@@ -200,6 +206,7 @@ def tile_input_masked_conv2d_kernel(tc, x, mask, weight, bias, out):
                 for n, i in enumerate(rows_of_kernel):
                     bank = 6 + (n if len(rows_of_kernel) == 2 else g % 2)
                     pts[(i, g)] = psum.tile([P, 2, 4, LINE], BF16, name="pt", tag="bank%d" % bank)
+                    keep_clock(pts[(i, g)][:].rearrange("p a s q -> p (a s q)"), 1)
                     for s in rows(i, g):
                         for a in range(2):
                             nc.tensor.transpose(pts[(i, g)][:, a, s % 4, :], xms[i][:, s % 4, a, :], ident[:])
@@ -250,10 +257,12 @@ def tile_input_masked_conv2d_kernel(tc, x, mask, weight, bias, out):
                 nc.sync.dma_start(out=out[b].rearrange("o y z -> o (y z)")[:, cols], in_=res[:])
 
         load_mask(0, 1)
-        load_x(0, 4)
-        load_x(1, 4)
+        load_x(0, 4, (0, 1))
+        load_mask(1, 2)
+        load_x(0, 4, (2, 3))
+        load_mask(2, 3)
+        load_x(1, 2, (0, 1))
         nc.sync.dma_start(out=w_raw[:], in_=weight.rearrange("o c i j -> o (c i j)"))
-        load_mask(1, 3)
         nc.vector.memset(m_rows[:], 0.0)
         for i in range(3):
             nc.sync.dma_start(
@@ -276,55 +285,60 @@ def tile_input_masked_conv2d_kernel(tc, x, mask, weight, bias, out):
         for q in range(4):
             regroup(True, 0, 8 * q, 8 * q + 8)
             multiply(0, 0, 0, 8 * q, 8 * q + 8)
-        for q in range(3):
-            regroup(False, 1, 8 * q, 8 * q + 8)
-        regroup(True, 1, 24, 32)
         nc.vector.tensor_copy(out=b_col[:], in_=b_bf[:])
-        load_x(2, 1)
-        load_x(3, 1)
+        load_x(2, 1, (0,))
 
         expand(1, 0, PIX)
-        weights(0)
-        weights(1)
         expand(2, 0, PIX)
+        for q in range(4):
+            regroup(False, 1, 8 * q, 8 * q + 8)
+        load_x(3, 1, (0,))
+        weights(0)
+        expand(3, 0, PIX)
+        weights(1)
+        expand(5, 0, PIX)
         weights(2)
         weights(3)
         weights(4)
         mask_columns()
-        expand(3, 0, PIX)
-        expand(5, 0, PIX)
         expand(6, 0, PIX)
-        scalar_way(SCALAR_WAY[0], 0)
         expand(7, 0, PIX)
         expand(8, 0, PIX)
+        scalar_way(SCALAR_WAY[0][0], 0)
         regroup(False, 2, 0, H)
         regroup(False, 3, 0, H)
+        scalar_way(SCALAR_WAY[1][0], 1)
 
         n = 0
         waiting = None
         for pair in range(2):
-            slow = [3 * i + 1 for i in SCALAR_WAY[pair]]
-            for k in [k for k in range(TAPS) if k not in slow]:
-                for b in (2 * pair, 2 * pair + 1):
-                    if n == 1:
-                        multiply(n % 3, k, b, 0, 16)
-                        multiply(n % 3, k, b, 16, H)
-                    elif n > 1:
-                        multiply(n % 3, k, b, 0, H)
-                    if waiting is not None:
-                        quantise(window(waiting[0], waiting[1]), waiting[1], waiting[2], 0, 1)
-                        matmul(waiting[1], waiting[2], 0)
-                        matmul(waiting[1], waiting[2], 1)
-                    waiting = (n % 3, k, b)
-                    n += 1
+            slow = [3 * i + 1 for job in SCALAR_WAY[pair] for i in job]
+            fast = [k for k in range(TAPS) if k not in slow]
+            both = (2 * pair, 2 * pair + 1)
+            if pair == 0:
+                order = [(k, b) for b in both for k in fast[0:3]] + [(k, b) for k in fast[3:] for b in both]
+            else:
+                order = [(k, b) for k in fast for b in both]
+            for k, b in order:
+                if n == 3:
+                    multiply(n % 3, k, b, 0, 16)
+                    multiply(n % 3, k, b, 16, H)
+                elif n > 0:
+                    multiply(n % 3, k, b, 0, H)
+                if waiting is not None:
+                    quantise(window(waiting[0], waiting[1]), waiting[1], waiting[2], 0, 1)
+                    matmul(waiting[1], waiting[2], 0)
+                    matmul(waiting[1], waiting[2], 1)
+                waiting = (n % 3, k, b)
+                n += 1
             quantise(window(waiting[0], waiting[1]), waiting[1], waiting[2], 0, 1)
             matmul(waiting[1], waiting[2], 0)
             matmul(waiting[1], waiting[2], 1)
             waiting = None
-            for i in SCALAR_WAY[pair]:
-                for b in (2 * pair, 2 * pair + 1):
+            for k in slow:
+                for b in both:
                     for h in range(2):
-                        quantise(big_window(i, b), 3 * i + 1, b, h, 2)
-                        matmul(3 * i + 1, b, h)
+                        quantise(big_window(k // 3, b), k, b, h, 2)
+                        matmul(k, b, h)
             if pair == 0:
-                scalar_way(SCALAR_WAY[1], 1)
+                scalar_way(SCALAR_WAY[1][1], 1)

@@ -23,7 +23,7 @@ XG = 4928
 BUF = (H + 2) * LINE
 FLOPS = 2 * B * COUT * CIN * TAPS * PIX
 
-SCALAR_WAY = (((1,),), ((0, 2), (1,)))
+SCALAR_WAY = (((1,),), ((0,), (1,)))
 
 
 def tile_input_masked_conv2d_kernel(tc, x, mask, weight, bias, out):
@@ -32,7 +32,7 @@ def tile_input_masked_conv2d_kernel(tc, x, mask, weight, bias, out):
         const = ctx.enter_context(tc.tile_pool(name="const", bufs=1))
         xr_pool = ctx.enter_context(tc.tile_pool(name="xr", bufs=2))
         xm_pool = ctx.enter_context(tc.tile_pool(name="xm", bufs=4))
-        code_pool = ctx.enter_context(tc.tile_pool(name="code", bufs=5))
+        code_pool = ctx.enter_context(tc.tile_pool(name="code", bufs=6))
         out_pool = ctx.enter_context(tc.tile_pool(name="outp", bufs=4))
         psum = ctx.enter_context(tc.psum_pool(name="psum", bufs=1))
 
@@ -45,7 +45,7 @@ def tile_input_masked_conv2d_kernel(tc, x, mask, weight, bias, out):
         xg = [const.tile([P, XG], BF16, name="xg%d" % b, align_bytes=64) for b in range(B)]
         prods = [const.tile([P, BUF], BF16, name="prod%d" % n, align_bytes=64) for n in range(3)]
         w_raw = const.tile([P, CIN * TAPS], BF16, name="w_raw", tag="g0", align_bytes=64)
-        wg = const.tile([P, TAPS * COUT * PACK], BF16, name="wg", tag="g2", align_bytes=64)
+        wg = const.tile([P, TAPS * COUT * PACK], BF16, name="wg", align_bytes=64)
         wc = const.tile([P, TAPS * COUT], U32, name="wc", align_bytes=64)
         ws = const.tile([P, TAPS * COUT], U8, name="ws", align_bytes=64)
         ident = const.tile([P, P], BF16, name="ident")
@@ -167,13 +167,8 @@ def tile_input_masked_conv2d_kernel(tc, x, mask, weight, bias, out):
             def rows(i, g):
                 return [s for s in range(4 * g, 4 * g + 4) if max(0, i - 1) <= s < min(H, H + i - 1)]
 
-            def keep_clock(bank, times):
-                for n in range(times):
-                    nc.tensor.matmul(out=bank[:, 0:256].bitcast(F32), lhsT=m_col[:], rhs=m_col[:], start=True, stop=True)
-
             def there(g):
                 xts[g] = psum.tile([P, 4, 2, P], BF16, name="xt", tag="bank%d" % (4 + g % 2))
-                keep_clock(xts[g][:].rearrange("p s a q -> p (s a q)"), (4 if g == 0 else len(rows_of_kernel)))
                 for s in range(4 * g, 4 * g + 4):
                     for a in range(2):
                         start = (s + 1) * ROW + 16
@@ -206,7 +201,6 @@ def tile_input_masked_conv2d_kernel(tc, x, mask, weight, bias, out):
                 for n, i in enumerate(rows_of_kernel):
                     bank = 6 + (n if len(rows_of_kernel) == 2 else g % 2)
                     pts[(i, g)] = psum.tile([P, 2, 4, LINE], BF16, name="pt", tag="bank%d" % bank)
-                    keep_clock(pts[(i, g)][:].rearrange("p a s q -> p (a s q)"), 1)
                     for s in rows(i, g):
                         for a in range(2):
                             nc.tensor.transpose(pts[(i, g)][:, a, s % 4, :], xms[i][:, s % 4, a, :], ident[:])
@@ -304,10 +298,9 @@ def tile_input_masked_conv2d_kernel(tc, x, mask, weight, bias, out):
         expand(6, 0, PIX)
         expand(7, 0, PIX)
         expand(8, 0, PIX)
-        scalar_way(SCALAR_WAY[0][0], 0)
         regroup(False, 2, 0, H)
+        scalar_way(SCALAR_WAY[0][0], 0)
         regroup(False, 3, 0, H)
-        scalar_way(SCALAR_WAY[1][0], 1)
 
         n = 0
         waiting = None
@@ -331,14 +324,22 @@ def tile_input_masked_conv2d_kernel(tc, x, mask, weight, bias, out):
                     matmul(waiting[1], waiting[2], 1)
                 waiting = (n % 3, k, b)
                 n += 1
+                if (k, b) == order[9] and len(slow) == 2:
+                    for bb in both:
+                        quantise(big_window(slow[0] // 3, bb), slow[0], bb, 0, 1)
+                        matmul(slow[0], bb, 0)
+                        matmul(slow[0], bb, 1)
             quantise(window(waiting[0], waiting[1]), waiting[1], waiting[2], 0, 1)
             matmul(waiting[1], waiting[2], 0)
             matmul(waiting[1], waiting[2], 1)
             waiting = None
-            for k in slow:
-                for b in both:
-                    for h in range(2):
-                        quantise(big_window(k // 3, b), k, b, h, 2)
-                        matmul(k, b, h)
+            k = slow[-1]
+            quantise(big_window(k // 3, both[0]), k, both[0], 0, 1)
+            matmul(k, both[0], 0)
+            matmul(k, both[0], 1)
+            for h in range(2):
+                quantise(big_window(k // 3, both[1]), k, both[1], h, 2)
+                matmul(k, both[1], h)
             if pair == 0:
-                scalar_way(SCALAR_WAY[1][1], 1)
+                for job in SCALAR_WAY[1]:
+                    scalar_way(job, 1)

@@ -23,7 +23,8 @@ XG = 4928
 BUF = (H + 2) * LINE
 FLOPS = 2 * B * COUT * CIN * TAPS * PIX
 
-SCALAR_WAY = (((1,),), ((0,), (1,)))
+SCALAR_WAY = ((1,), (1, 0))
+SHARED_FROM = 4
 
 
 def tile_input_masked_conv2d_kernel(tc, x, mask, weight, bias, out):
@@ -32,7 +33,7 @@ def tile_input_masked_conv2d_kernel(tc, x, mask, weight, bias, out):
         const = ctx.enter_context(tc.tile_pool(name="const", bufs=1))
         xr_pool = ctx.enter_context(tc.tile_pool(name="xr", bufs=2))
         xm_pool = ctx.enter_context(tc.tile_pool(name="xm", bufs=4))
-        code_pool = ctx.enter_context(tc.tile_pool(name="code", bufs=6))
+        code_pool = ctx.enter_context(tc.tile_pool(name="code", bufs=5))
         out_pool = ctx.enter_context(tc.tile_pool(name="outp", bufs=4))
         psum = ctx.enter_context(tc.psum_pool(name="psum", bufs=1))
 
@@ -45,7 +46,7 @@ def tile_input_masked_conv2d_kernel(tc, x, mask, weight, bias, out):
         xg = [const.tile([P, XG], BF16, name="xg%d" % b, align_bytes=64) for b in range(B)]
         prods = [const.tile([P, BUF], BF16, name="prod%d" % n, align_bytes=64) for n in range(3)]
         w_raw = const.tile([P, CIN * TAPS], BF16, name="w_raw", tag="g0", align_bytes=64)
-        wg = const.tile([P, TAPS * COUT * PACK], BF16, name="wg", align_bytes=64)
+        wg = const.tile([P, TAPS * COUT * PACK], BF16, name="wg", tag="g2", align_bytes=64)
         wc = const.tile([P, TAPS * COUT], U32, name="wc", align_bytes=64)
         ws = const.tile([P, TAPS * COUT], U8, name="ws", align_bytes=64)
         ident = const.tile([P, P], BF16, name="ident")
@@ -63,13 +64,12 @@ def tile_input_masked_conv2d_kernel(tc, x, mask, weight, bias, out):
 
         xr = []
 
-        def load_x(b, chunks, which):
-            if len(xr) == b:
-                xr.append(xr_pool.tile([P, PACK, PIX], BF16, name="xr"))
-            t = xr[b]
+        def load_x(b, chunks):
+            t = xr_pool.tile([P, PACK, PIX], BF16, name="xr")
+            xr.append(t)
             src = x[b].rearrange("(p t) y z -> p t (y z)", t=PACK)
             step = PIX // chunks
-            for c in which:
+            for c in range(chunks):
                 nc.sync.dma_start(
                     out=t[:, :, c * step : (c + 1) * step],
                     in_=src[:, :, c * step : (c + 1) * step],
@@ -95,11 +95,13 @@ def tile_input_masked_conv2d_kernel(tc, x, mask, weight, bias, out):
             else:
                 nc.scalar.copy(out=dst, in_=src)
 
-        def expand(k, n0, n1):
-            nc.scalar.copy(
-                out=me[k][:, n0 * 2 : n1 * 2].rearrange("p (n e) -> p n e", e=2),
-                in_=mb[:, k * PIX + n0 : k * PIX + n1].unsqueeze(2).to_broadcast([P, n1 - n0, 2]),
-            )
+        def expand(k, n0, n1, on_vector=False):
+            dst = me[k][:, n0 * 2 : n1 * 2].rearrange("p (n e) -> p n e", e=2)
+            src = mb[:, k * PIX + n0 : k * PIX + n1].unsqueeze(2).to_broadcast([P, n1 - n0, 2])
+            if on_vector:
+                nc.vector.tensor_copy(out=dst, in_=src)
+            else:
+                nc.scalar.copy(out=dst, in_=src)
 
         w4 = w_raw[:].rearrange("o (p t k) -> o p t k", t=PACK, k=TAPS)
 
@@ -133,11 +135,12 @@ def tile_input_masked_conv2d_kernel(tc, x, mask, weight, bias, out):
 
         def multiply(n, k, b, y0, y1):
             i, j = k // 3, k % 3
+            dst = prods[n] if n >= 0 else big[i][:, b % 2, :]
             y0 = max(y0, 1 - i)
             y1 = min(y1, H + 1 - i)
             off = i * ROW + (3 + j) * PACK
             nc.vector.tensor_tensor(
-                out=prods[n][:, (i + y0) * LINE : (i + y1) * LINE].rearrange(
+                out=dst[:, (i + y0) * LINE : (i + y1) * LINE].rearrange(
                     "p (y z r e) -> p y z r e", z=W, r=2, e=2
                 ),
                 in0=xg[b][:, off + y0 * ROW : off + y1 * ROW]
@@ -152,7 +155,7 @@ def tile_input_masked_conv2d_kernel(tc, x, mask, weight, bias, out):
 
         big = {}
 
-        def scalar_way(rows_of_kernel, pair):
+        def scalar_way(rows_of_kernel, pair, first=0):
             for i in rows_of_kernel:
                 if i not in big:
                     big[i] = const.tile([P, 2, BUF], BF16, name="big%d" % i, tag="g%d" % i, align_bytes=64)
@@ -184,8 +187,8 @@ def tile_input_masked_conv2d_kernel(tc, x, mask, weight, bias, out):
                         in_=pts[(i, g)][:, :, r[0] % 4 : r[-1] % 4 + 1, :],
                     )
 
-            there(0)
-            for g in range(groups):
+            there(first)
+            for g in range(first, groups):
                 if g + 1 < groups:
                     there(g + 1)
                 xms = {}
@@ -196,7 +199,7 @@ def tile_input_masked_conv2d_kernel(tc, x, mask, weight, bias, out):
                         nc.scalar.activation(
                             out=xms[i][:, s % 4, :, :], in_=xts[g][:, s % 4, :, :], func=COPY, scale=m_col[:, col : col + 1]
                         )
-                if g > 0:
+                if g > first:
                     leave(g - 1)
                 for n, i in enumerate(rows_of_kernel):
                     bank = 6 + (n if len(rows_of_kernel) == 2 else g % 2)
@@ -251,12 +254,10 @@ def tile_input_masked_conv2d_kernel(tc, x, mask, weight, bias, out):
                 nc.sync.dma_start(out=out[b].rearrange("o y z -> o (y z)")[:, cols], in_=res[:])
 
         load_mask(0, 1)
-        load_x(0, 4, (0, 1))
-        load_mask(1, 2)
-        load_x(0, 4, (2, 3))
-        load_mask(2, 3)
-        load_x(1, 2, (0, 1))
+        load_x(0, 4)
+        load_x(1, 4)
         nc.sync.dma_start(out=w_raw[:], in_=weight.rearrange("o c i j -> o (c i j)"))
+        load_mask(1, 3)
         nc.vector.memset(m_rows[:], 0.0)
         for i in range(3):
             nc.sync.dma_start(
@@ -275,71 +276,70 @@ def tile_input_masked_conv2d_kernel(tc, x, mask, weight, bias, out):
             nc.vector.memset(prods[n][:, (H + 1) * LINE : BUF], 0.0)
 
         for q in range(4):
-            expand(0, 256 * q, 256 * q + 256)
+            expand(0, 256 * q, 256 * q + 256, q < 2)
         for q in range(4):
             regroup(True, 0, 8 * q, 8 * q + 8)
             multiply(0, 0, 0, 8 * q, 8 * q + 8)
+        for q in range(3):
+            regroup(False, 1, 8 * q, 8 * q + 8)
+        regroup(True, 1, 24, 32)
         nc.vector.tensor_copy(out=b_col[:], in_=b_bf[:])
-        load_x(2, 1, (0,))
+        load_x(2, 1)
+        load_x(3, 1)
 
         expand(1, 0, PIX)
-        expand(2, 0, PIX)
-        for q in range(4):
-            regroup(False, 1, 8 * q, 8 * q + 8)
-        load_x(3, 1, (0,))
         weights(0)
-        expand(3, 0, PIX)
         weights(1)
-        expand(5, 0, PIX)
+        expand(2, 0, PIX)
         weights(2)
         weights(3)
         weights(4)
         mask_columns()
+        expand(3, 0, PIX)
+        expand(5, 0, PIX)
         expand(6, 0, PIX)
+        scalar_way(SCALAR_WAY[0], 0)
         expand(7, 0, PIX)
         expand(8, 0, PIX)
         regroup(False, 2, 0, H)
-        scalar_way(SCALAR_WAY[0][0], 0)
         regroup(False, 3, 0, H)
 
         n = 0
         waiting = None
         for pair in range(2):
-            slow = [3 * i + 1 for job in SCALAR_WAY[pair] for i in job]
-            fast = [k for k in range(TAPS) if k not in slow]
-            both = (2 * pair, 2 * pair + 1)
-            if pair == 0:
-                order = [(k, b) for b in both for k in fast[0:3]] + [(k, b) for k in fast[3:] for b in both]
-            else:
-                order = [(k, b) for k in fast for b in both]
-            for k, b in order:
-                if n == 3:
-                    multiply(n % 3, k, b, 0, 16)
-                    multiply(n % 3, k, b, 16, H)
-                elif n > 0:
-                    multiply(n % 3, k, b, 0, H)
-                if waiting is not None:
-                    quantise(window(waiting[0], waiting[1]), waiting[1], waiting[2], 0, 1)
-                    matmul(waiting[1], waiting[2], 0)
-                    matmul(waiting[1], waiting[2], 1)
-                waiting = (n % 3, k, b)
-                n += 1
-                if (k, b) == order[9] and len(slow) == 2:
-                    for bb in both:
-                        quantise(big_window(slow[0] // 3, bb), slow[0], bb, 0, 1)
-                        matmul(slow[0], bb, 0)
-                        matmul(slow[0], bb, 1)
+            slow = [3 * i + 1 for i in SCALAR_WAY[pair]]
+            if pair == 1:
+                slow.append(7)
+            for k in [k for k in range(TAPS) if k not in slow]:
+                for b in (2 * pair, 2 * pair + 1):
+                    if n == 1:
+                        multiply(n % 3, k, b, 0, 16)
+                        multiply(n % 3, k, b, 16, H)
+                    elif n > 1:
+                        multiply(n % 3, k, b, 0, H)
+                    if waiting is not None:
+                        quantise(window(waiting[0], waiting[1]), waiting[1], waiting[2], 0, 1)
+                        matmul(waiting[1], waiting[2], 0)
+                        matmul(waiting[1], waiting[2], 1)
+                    waiting = (n % 3, k, b)
+                    n += 1
+            if pair == 1:
+                for b in (2, 3):
+                    multiply(-1, 7, b, 0, 4 * SHARED_FROM - 1)
             quantise(window(waiting[0], waiting[1]), waiting[1], waiting[2], 0, 1)
             matmul(waiting[1], waiting[2], 0)
             matmul(waiting[1], waiting[2], 1)
             waiting = None
-            k = slow[-1]
-            quantise(big_window(k // 3, both[0]), k, both[0], 0, 1)
-            matmul(k, both[0], 0)
-            matmul(k, both[0], 1)
-            for h in range(2):
-                quantise(big_window(k // 3, both[1]), k, both[1], h, 2)
-                matmul(k, both[1], h)
+            for k in slow:
+                for b in (2 * pair, 2 * pair + 1):
+                    parts = 2 if (k, b) == (slow[-1], 2 * pair + 1) else 1
+                    for part in range(parts):
+                        quantise(big_window(k // 3, b), k, b, part, parts)
+                        if parts == 2:
+                            matmul(k, b, part)
+                    if parts == 1:
+                        matmul(k, b, 0)
+                        matmul(k, b, 1)
             if pair == 0:
-                for job in SCALAR_WAY[1]:
-                    scalar_way(job, 1)
+                scalar_way(SCALAR_WAY[1], 1)
+                scalar_way((2,), 1, SHARED_FROM)

from contextlib import ExitStack

import concourse.mybir as mybir
from concourse.masks import make_identity

BF16 = mybir.dt.bfloat16
F32 = mybir.dt.float32
U32 = mybir.dt.uint32
U8 = mybir.dt.uint8
FP8X4 = mybir.dt.float8_e4m3fn_x4
MULT = mybir.AluOpType.mult
IDENT = mybir.ActivationFunctionType.Identity
COPY = mybir.ActivationFunctionType.Copy

P = 128
B, CIN, COUT, H, W = 4, 512, 128, 32, 32
TAPS = 9
PIX = H * W
PACK = 4
LINE = W * PACK
ROW = (W + 4) * PACK
XG = 4928
BUF = (H + 2) * LINE
FLOPS = 2 * B * COUT * CIN * TAPS * PIX

SCALAR_WAY = ((1,), (1, 0))
SHARED_FROM = 4


def tile_input_masked_conv2d_kernel(tc, x, mask, weight, bias, out):
    nc = tc.nc
    with ExitStack() as ctx:
        const = ctx.enter_context(tc.tile_pool(name="const", bufs=1))
        xr_pool = ctx.enter_context(tc.tile_pool(name="xr", bufs=2))
        xm_pool = ctx.enter_context(tc.tile_pool(name="xm", bufs=4))
        code_pool = ctx.enter_context(tc.tile_pool(name="code", bufs=5))
        out_pool = ctx.enter_context(tc.tile_pool(name="outp", bufs=4))
        psum = ctx.enter_context(tc.psum_pool(name="psum", bufs=1))

        mask_flat = mask.rearrange("a k n -> (a k n)")
        mb = const.tile([P, TAPS * PIX], BF16, name="mb")
        me = {}
        for k in range(TAPS):
            if k != 4:
                me[k] = const.tile([P, PIX * 2], BF16, name="me%d" % k)
        xg = [const.tile([P, XG], BF16, name="xg%d" % b, align_bytes=64) for b in range(B)]
        prods = [const.tile([P, BUF], BF16, name="prod%d" % n, align_bytes=64) for n in range(3)]
        w_raw = const.tile([P, CIN * TAPS], BF16, name="w_raw", tag="g0", align_bytes=64)
        wg = const.tile([P, TAPS * COUT * PACK], BF16, name="wg", tag="g2", align_bytes=64)
        wc = const.tile([P, TAPS * COUT], U32, name="wc", align_bytes=64)
        ws = const.tile([P, TAPS * COUT], U8, name="ws", align_bytes=64)
        ident = const.tile([P, P], BF16, name="ident")
        b_bf = const.tile([P, 1], BF16, name="b_bf")
        b_col = const.tile([P, 1], F32, name="b_col")
        m_rows = const.tile([P, W], BF16, name="m_rows")
        m_wide = const.tile([P, LINE], BF16, name="m_wide")
        m_col = const.tile([P, P], F32, name="m_col")

        def load_mask(k0, k1):
            nc.sync.dma_start(
                out=mb[:, k0 * PIX : k1 * PIX],
                in_=mask_flat[k0 * PIX : k1 * PIX].partition_broadcast(P),
            )

        xr = []

        def load_x(b, chunks):
            t = xr_pool.tile([P, PACK, PIX], BF16, name="xr")
            xr.append(t)
            src = x[b].rearrange("(p t) y z -> p t (y z)", t=PACK)
            step = PIX // chunks
            for c in range(chunks):
                nc.sync.dma_start(
                    out=t[:, :, c * step : (c + 1) * step],
                    in_=src[:, :, c * step : (c + 1) * step],
                )

        def zero_pads(b):
            t = xg[b]
            nc.vector.memset(
                t[:, 0 : (H + 2) * ROW].rearrange("p (y r) -> p y r", r=ROW)[:, :, 0:16], 0.0
            )
            nc.vector.memset(t[:, 16:ROW], 0.0)
            nc.vector.memset(t[:, (H + 1) * ROW + 16 : XG], 0.0)

        def regroup(on_vector, b, y0, y1):
            dst = (
                xg[b][:, ROW + 16 + y0 * ROW : ROW + 16 + y1 * ROW]
                .rearrange("p (y r) -> p y r", r=ROW)[:, :, 0:LINE]
                .rearrange("p y (z t) -> p y z t", t=PACK)
            )
            src = xr[b][:, :, y0 * W : y1 * W].rearrange("p t (y z) -> p y z t", z=W)
            if on_vector:
                nc.vector.tensor_copy(out=dst, in_=src)
            else:
                nc.scalar.copy(out=dst, in_=src)

        def expand(k, n0, n1, on_vector=False):
            dst = me[k][:, n0 * 2 : n1 * 2].rearrange("p (n e) -> p n e", e=2)
            src = mb[:, k * PIX + n0 : k * PIX + n1].unsqueeze(2).to_broadcast([P, n1 - n0, 2])
            if on_vector:
                nc.vector.tensor_copy(out=dst, in_=src)
            else:
                nc.scalar.copy(out=dst, in_=src)

        w4 = w_raw[:].rearrange("o (p t k) -> o p t k", t=PACK, k=TAPS)

        def weights(g):
            taps = [k for k in (2 * g, 2 * g + 1) if k < TAPS]
            n = len(taps)
            wt = psum.tile([P, 2 * PACK, COUT], BF16, name="wt", tag="bank%d" % (4 + g % 4))
            for a, k in enumerate(taps):
                for t in range(PACK):
                    nc.tensor.transpose(wt[:, a * PACK + t, :], w4[:, :, t, k], ident[:])
            lo = 2 * g * COUT * PACK
            hi = lo + n * COUT * PACK
            nc.scalar.copy(
                out=wg[:, lo:hi].rearrange("p (a o t) -> p a o t", a=n, t=PACK),
                in_=wt[:, 0 : n * PACK, :].rearrange("p (a t) o -> p a o t", t=PACK),
            )
            nc.vector.quantize_mx(
                out=wc[:, lo // PACK : hi // PACK].bitcast(FP8X4),
                scales=ws[:, lo // PACK : hi // PACK],
                in_=wg[:, lo:hi],
            )

        def mask_columns():
            nc.vector.tensor_copy(
                out=m_wide[:].rearrange("p (z t) -> p z t", t=PACK),
                in_=m_rows[:].unsqueeze(2).to_broadcast([P, W, PACK]),
            )
            mt = psum.tile([P, P], BF16, name="mt", tag="bank5")
            nc.tensor.transpose(mt[:], m_wide[:], ident[:])
            nc.vector.tensor_copy(out=m_col[:], in_=mt[:])

        def multiply(n, k, b, y0, y1):
            i, j = k // 3, k % 3
            dst = prods[n] if n >= 0 else big[i][:, b % 2, :]
            y0 = max(y0, 1 - i)
            y1 = min(y1, H + 1 - i)
            off = i * ROW + (3 + j) * PACK
            nc.vector.tensor_tensor(
                out=dst[:, (i + y0) * LINE : (i + y1) * LINE].rearrange(
                    "p (y z r e) -> p y z r e", z=W, r=2, e=2
                ),
                in0=xg[b][:, off + y0 * ROW : off + y1 * ROW]
                .rearrange("p (y q) -> p y q", q=ROW)[:, :, 0:LINE]
                .rearrange("p y (z r e) -> p y z r e", r=2, e=2),
                in1=me[k][:, y0 * W * 2 : y1 * W * 2]
                .rearrange("p (y z e) -> p y z e", z=W, e=2)
                .unsqueeze(3)
                .to_broadcast([P, y1 - y0, W, 2, 2]),
                op=MULT,
            )

        big = {}

        def scalar_way(rows_of_kernel, pair, first=0):
            for i in rows_of_kernel:
                if i not in big:
                    big[i] = const.tile([P, 2, BUF], BF16, name="big%d" % i, tag="g%d" % i, align_bytes=64)
                    if i == 0:
                        nc.vector.memset(big[i][:, :, 0:LINE], 0.0)
                    if i == 2:
                        nc.vector.memset(big[i][:, :, (H + 1) * LINE : BUF], 0.0)
            groups = H // 4
            xts = {}
            pts = {}

            def rows(i, g):
                return [s for s in range(4 * g, 4 * g + 4) if max(0, i - 1) <= s < min(H, H + i - 1)]

            def there(g):
                xts[g] = psum.tile([P, 4, 2, P], BF16, name="xt", tag="bank%d" % (4 + g % 2))
                for s in range(4 * g, 4 * g + 4):
                    for a in range(2):
                        start = (s + 1) * ROW + 16
                        nc.tensor.transpose(xts[g][:, s % 4, a, :], xg[2 * pair + a][:, start : start + LINE], ident[:])

            def leave(g):
                for n, i in enumerate(rows_of_kernel):
                    r = rows(i, g)
                    nc.scalar.copy(
                        out=big[i][:, :, (r[0] + 1) * LINE : (r[-1] + 2) * LINE].rearrange(
                            "p a (s q) -> p a s q", q=LINE
                        ),
                        in_=pts[(i, g)][:, :, r[0] % 4 : r[-1] % 4 + 1, :],
                    )

            there(first)
            for g in range(first, groups):
                if g + 1 < groups:
                    there(g + 1)
                xms = {}
                for i in rows_of_kernel:
                    xms[i] = xm_pool.tile([P, 4, 2, P], BF16, name="xm")
                    for s in rows(i, g):
                        col = 32 * i + s - i + 1
                        nc.scalar.activation(
                            out=xms[i][:, s % 4, :, :], in_=xts[g][:, s % 4, :, :], func=COPY, scale=m_col[:, col : col + 1]
                        )
                if g > first:
                    leave(g - 1)
                for n, i in enumerate(rows_of_kernel):
                    bank = 6 + (n if len(rows_of_kernel) == 2 else g % 2)
                    pts[(i, g)] = psum.tile([P, 2, 4, LINE], BF16, name="pt", tag="bank%d" % bank)
                    for s in rows(i, g):
                        for a in range(2):
                            nc.tensor.transpose(pts[(i, g)][:, a, s % 4, :], xms[i][:, s % 4, a, :], ident[:])
            leave(groups - 1)

        acc = {}
        held = {}
        passes = {}

        def quantise(src, k, b, part, parts):
            if part == 0:
                codes = code_pool.tile([P, PIX], U32, name="codes", align_bytes=64)
                scl = code_pool.tile([P, PIX], U8, name="scl", align_bytes=64)
                held[(k, b)] = (codes, scl)
            codes, scl = held[(k, b)]
            wid = PIX // parts
            nc.vector.quantize_mx(
                out=codes[:, part * wid : (part + 1) * wid].bitcast(FP8X4),
                scales=scl[:, part * wid : (part + 1) * wid],
                in_=src[:, part * wid * PACK : (part + 1) * wid * PACK],
            )

        def window(n, k):
            return prods[n][:, (k // 3) * LINE : (k // 3 + H) * LINE]

        def big_window(i, b):
            return big[i][:, b % 2, i * LINE : (i + H) * LINE]

        def matmul(k, b, h):
            codes, scl = held[(k, b)]
            seen = passes.get((b, h), 0)
            passes[(b, h)] = seen + 1
            if seen == 0:
                acc[(b, h)] = psum.tile([P, 512], F32, name="acc", tag="bank%d" % (2 * (b % 2) + h))
            cols = slice(h * 512, (h + 1) * 512)
            nc.tensor.matmul_mx(
                out=acc[(b, h)][:],
                lhsT=wc[:, k * COUT : (k + 1) * COUT].bitcast(FP8X4),
                lhsT_scale=ws[:, k * COUT : (k + 1) * COUT],
                rhs=codes[:, cols].bitcast(FP8X4),
                rhs_scale=scl[:, cols],
                start=(seen == 0),
                stop=(seen == TAPS - 1),
            )
            if seen == TAPS - 1:
                res = out_pool.tile([P, 512], F32, name="res")
                nc.scalar.activation(out=res[:], in_=acc[(b, h)][:], func=IDENT, bias=b_col[:, 0:1], scale=1.0)
                nc.sync.dma_start(out=out[b].rearrange("o y z -> o (y z)")[:, cols], in_=res[:])

        load_mask(0, 1)
        load_x(0, 4)
        load_x(1, 4)
        nc.sync.dma_start(out=w_raw[:], in_=weight.rearrange("o c i j -> o (c i j)"))
        load_mask(1, 3)
        nc.vector.memset(m_rows[:], 0.0)
        for i in range(3):
            nc.sync.dma_start(
                out=m_rows[32 * i : 32 * i + 32, :],
                in_=mask_flat[(3 * i + 1) * PIX : (3 * i + 2) * PIX].rearrange("(y z) -> y z", z=W),
            )
        load_mask(3, TAPS)
        with nc.allow_non_contiguous_dma(reason="128 bias values, one to a partition"):
            nc.sync.dma_start(out=b_bf[:], in_=bias.rearrange("(o u) -> o u", u=1))

        make_identity(nc, ident[:])
        for b in range(B):
            zero_pads(b)
        for n in range(3):
            nc.vector.memset(prods[n][:, 0:LINE], 0.0)
            nc.vector.memset(prods[n][:, (H + 1) * LINE : BUF], 0.0)

        for q in range(4):
            expand(0, 256 * q, 256 * q + 256, q < 2)
        for q in range(4):
            regroup(True, 0, 8 * q, 8 * q + 8)
            multiply(0, 0, 0, 8 * q, 8 * q + 8)
        for q in range(3):
            regroup(False, 1, 8 * q, 8 * q + 8)
        regroup(True, 1, 24, 32)
        nc.vector.tensor_copy(out=b_col[:], in_=b_bf[:])
        load_x(2, 1)
        load_x(3, 1)

        expand(1, 0, PIX)
        weights(0)
        weights(1)
        expand(2, 0, PIX)
        weights(2)
        weights(3)
        weights(4)
        mask_columns()
        expand(3, 0, PIX)
        expand(5, 0, PIX)
        expand(6, 0, PIX)
        scalar_way(SCALAR_WAY[0], 0)
        expand(7, 0, PIX)
        expand(8, 0, PIX)
        regroup(False, 2, 0, H)
        regroup(False, 3, 0, H)

        n = 0
        waiting = None
        for pair in range(2):
            slow = [3 * i + 1 for i in SCALAR_WAY[pair]]
            if pair == 1:
                slow.append(7)
            for k in [k for k in range(TAPS) if k not in slow]:
                for b in (2 * pair, 2 * pair + 1):
                    if n == 1:
                        multiply(n % 3, k, b, 0, 16)
                        multiply(n % 3, k, b, 16, H)
                    elif n > 1:
                        multiply(n % 3, k, b, 0, H)
                    if waiting is not None:
                        quantise(window(waiting[0], waiting[1]), waiting[1], waiting[2], 0, 1)
                        matmul(waiting[1], waiting[2], 0)
                        matmul(waiting[1], waiting[2], 1)
                    waiting = (n % 3, k, b)
                    n += 1
            if pair == 1:
                for b in (2, 3):
                    multiply(-1, 7, b, 0, 4 * SHARED_FROM - 1)
            quantise(window(waiting[0], waiting[1]), waiting[1], waiting[2], 0, 1)
            matmul(waiting[1], waiting[2], 0)
            matmul(waiting[1], waiting[2], 1)
            waiting = None
            for k in slow:
                for b in (2 * pair, 2 * pair + 1):
                    parts = 2 if (k, b) == (slow[-1], 2 * pair + 1) else 1
                    for part in range(parts):
                        quantise(big_window(k // 3, b), k, b, part, parts)
                        if parts == 2:
                            matmul(k, b, part)
                    if parts == 1:
                        matmul(k, b, 0)
                        matmul(k, b, 1)
            if pair == 0:
                scalar_way(SCALAR_WAY[1], 1)
                scalar_way((2,), 1, SHARED_FROM)
